import numpy as np
import ml_dtypes


def mxq(x, axis, fmt="e4m3"):
    dtype, down = {"e4m3": (ml_dtypes.float8_e4m3fn, 7), "e5m2": (ml_dtypes.float8_e5m2, 14)}[fmt]
    v = np.moveaxis(np.asarray(x, np.float32).astype(ml_dtypes.bfloat16).astype(np.float64), axis, -1)
    blocks = v.reshape(v.shape[:-1] + (-1, 32))
    amax = np.abs(blocks).max(-1, keepdims=True)
    byte = np.maximum(np.where(amax > 0, np.frexp(amax)[1] - 1 + 127, 0) - down, 1)
    scale = np.exp2(byte - 127.0)
    codes = (blocks / scale).astype(np.float32).astype(dtype).astype(np.float64)
    return np.moveaxis((codes * scale).reshape(v.shape), -1, axis)


WIDE = False


def mx_kscale(k):
    if not WIDE:
        return np.ones(k)
    levels = np.array([18, -18])
    if k % 512:
        return np.exp2(np.random.permutation(np.resize(levels, k // 32))).repeat(32)
    a = np.empty((k // 512, 16))
    for p in range(k // 512):
        a[p, :8] = np.random.permutation(np.resize(levels, 8))
        for g in range(8):
            far = levels[np.abs(levels - a[p, g]) >= 10]
            a[p, g + 8] = far[np.random.randint(len(far))]
    return np.exp2(a.ravel()).repeat(32)


BF16 = ml_dtypes.bfloat16


def bf(x):
    return np.asarray(x, np.float32).astype(BF16)


def f64(x):
    return np.asarray(x).astype(np.float64)


N, D, K = 2048, 512, 1024
SX, SO = 0.5, 0.25
LN2PI_2 = np.log(2.0 * np.pi) / 2.0


def setup_inputs():
    s = mx_kscale(N)[:, None]
    u = mx_kscale(K)
    c = SO * np.random.standard_normal(D)
    x = bf((SX * np.random.standard_normal((N, D)) + c) * s)
    means = bf((c + 0.1 * np.random.standard_normal((K, D))) * np.min(s))
    vars_ = bf(SX * SX * np.exp(0.5 * np.random.standard_normal((K, D))) * u[:, None])
    g = bf(0.25 * np.random.standard_normal((N, K)) * np.exp2(np.random.randint(-6, 1, (N, 1))) / s * u)
    return {"x": x, "means": means, "vars_": vars_, "grad_out": g}


def reference(x, means, vars_, grad_out):
    x, m, v, g = f64(x), f64(means), f64(vars_), f64(grad_out)
    inv_v = 1.0 / v
    w2 = mxq(np.concatenate([inv_v, m * inv_v], axis=1), 0, "e4m3")
    ab = mxq(g, 1, "e5m2") @ w2
    dx = ab[:, D:] - x * ab[:, :D]
    gx = mxq(g, 0, "e5m2").T @ mxq(x, 0, "e4m3")
    dm = inv_v * (gx - m * np.sum(g, axis=0)[:, None])
    return dx, dm

@@ -1,0 +1,410 @@
+from contextlib import ExitStack
+
+import concourse.mybir as mybir
+from concourse.masks import make_identity
+
+N, D, K = 2048, 512, 1024
+FLOPS = 2 * N * K * 2 * D + 2 * K * N * D
+
+F32 = mybir.dt.float32
+BF16 = mybir.dt.bfloat16
+U32 = mybir.dt.uint32
+U8 = mybir.dt.uint8
+E4 = mybir.dt.float8_e4m3fn_x4
+E5 = mybir.dt.float8_e5m2_x4
+ALU = mybir.AluOpType
+ACT = mybir.ActivationFunctionType
+
+P = 128
+PACK = 4
+ROW_PASSES = N // (P * PACK)
+K_PASSES = K // (P * PACK)
+CHUNKS = 4
+CW = D // CHUNKS
+SUM_N = 32
+
+
+def tile_gmm_pb_v_kernel(tc, x, means, vars_, grad_out, out_0, out_1):
+    nc = tc.nc
+    x_h = x.rearrange("(s p j) d -> s p j d", p=P, j=PACK)
+    g_h = grad_out.rearrange("(s p j) k -> s p j k", p=P, j=PACK)
+    m_h = means.rearrange("(s p j) d -> s p j d", p=P, j=PACK)
+    v_h = vars_.rearrange("(s p j) d -> s p j d", p=P, j=PACK)
+    dx_h = out_0.rearrange("(s p j) d -> s p j d", p=P, j=PACK)
+    dm_h = out_1.rearrange("(s p j) d -> s p j d", p=P, j=PACK)
+
+    with ExitStack() as ctx:
+        keep = ctx.enter_context(tc.tile_pool(name="keep", bufs=1))
+        psum = ctx.enter_context(tc.psum_pool(name="psum", bufs=1))
+        ctx.enter_context(tc.manual_schedule())
+
+        def bank(b, name):
+            return psum.tile([P, 512], F32, tag="bank%d" % b, name=name)
+
+        def kept(shape, dtype, name):
+            return keep.tile(shape, dtype, name=name, align_bytes=64)
+
+        def ring(shape, dtype, tag, bufs, name):
+            return keep.tile(shape, dtype, tag=tag, bufs=bufs, name=name, align_bytes=64)
+
+        v_raw = [kept([P, PACK, D], BF16, "v_raw%d" % s) for s in range(K_PASSES)]
+        m_raw = [kept([P, PACK, D], BF16, "m_raw%d" % s) for s in range(K_PASSES)]
+        g_raw = [kept([P, PACK, K], BF16, "g_raw%d" % s) for s in range(ROW_PASSES)]
+        x_raw = [kept([P, PACK, D], BF16, "x_raw%d" % s) for s in range(ROW_PASSES)]
+        inv = [kept([P, CHUNKS, PACK, CW], F32, "inv%d" % s) for s in range(K_PASSES)]
+
+        for tiles, view, s in (
+            (v_raw, v_h, 0), (m_raw, m_h, 0), (v_raw, v_h, 1), (g_raw, g_h, 0), (m_raw, m_h, 1),
+            (g_raw, g_h, 1), (x_raw, x_h, 0), (g_raw, g_h, 2), (g_raw, g_h, 3),
+            (x_raw, x_h, 1), (x_raw, x_h, 2), (x_raw, x_h, 3),
+        ):
+            nc.sync.dma_start(out=tiles[s][:], in_=view[s])
+
+        ident = kept([P, P], F32, "ident")
+        ones_f = kept([P, SUM_N], F32, "ones_f")
+        ones = kept([P, SUM_N], BF16, "ones")
+        pick = kept([P, PACK, 4, 32], F32, "pick")
+        nc.vector.memset(ones_f[:], 1.0)
+        nc.scalar.activation(out=ones[:], in_=ones_f[:], func=ACT.Abs_reciprocal_sqrt)
+        make_identity(nc, ident[:])
+        for q in range(4):
+            nc.vector.tensor_scalar(
+                out=pick[:, :, q, :], in0=ident[:].rearrange("p (m j) -> p j m", j=PACK),
+                scalar1=-1.0, scalar2=None, op0=ALU.mult,
+            )
+
+        def quantize(staged, fmt, name):
+            codes = kept([P, 512], U32, name + "_codes")
+            scales = kept([P, 512], U8, name + "_scales")
+            nc.vector.quantize_mx(out=codes[:].bitcast(fmt), scales=scales[:], in_=staged[:])
+            return codes, scales
+
+        sum_banks = {}
+
+        def column_sums(s):
+            if s % 2 == 0:
+                sum_banks[s // 2] = bank(6 + s // 2, "sums%d" % (s // 2))
+            acc = sum_banks[s // 2]
+            for b in range(8):
+                c0 = ((s % 2) * 8 + b) * SUM_N
+                for j in range(PACK):
+                    nc.tensor.matmul(
+                        acc[:, c0 : c0 + SUM_N], lhsT=g_raw[s][:, j, b * P : (b + 1) * P], rhs=ones[:],
+                        start=(j == 0), stop=(j == PACK - 1),
+                    )
+
+        part_sums = kept([P, 32], F32, "part_sums")
+        neg_g = kept([P, K_PASSES, PACK], F32, "neg_g")
+        picked = {}
+
+        def copy_sums():
+            for h in range(2):
+                nc.scalar.copy(out=part_sums[:, 16 * h : 16 * (h + 1)], in_=sum_banks[h][:, 0:512:SUM_N])
+
+        def permute_sums():
+            picked[0] = bank(6, "picked")
+            for j in range(PACK):
+                nc.tensor.matmul(
+                    picked[0][:, 32 * j : 32 * (j + 1)],
+                    lhsT=pick[:, j, :, :].rearrange("p q m -> p (q m)"), rhs=part_sums[:], start=True, stop=True,
+                )
+
+        def reduce_sums():
+            view = picked[0][:, 0:128].rearrange("p (j s g q) -> p q g j s", j=PACK, s=ROW_PASSES, g=K_PASSES)
+            for q in range(4):
+                rows = slice(32 * q, 32 * (q + 1))
+                nc.vector.tensor_reduce(
+                    out=neg_g[rows, :, :], in_=view[rows, q, :, :, :], axis=mybir.AxisListType.X, op=ALU.add
+                )
+
+        turned = {}
+        f_stage = {}
+        f_mx = {}
+
+        def transpose_tile(s, j, b):
+            turned[s, j] = bank(b, "turned%d_%d" % (s, j))
+            words = g_raw[s][:, j, :].bitcast(F32)
+            for g in range(K_PASSES):
+                for u in range(2):
+                    c0 = (2 * g + u) * P
+                    nc.tensor.transpose(
+                        turned[s, j][:, c0 : c0 + P], words[:, 256 * g + u : 256 * (g + 1) : 2], ident[:]
+                    )
+
+        def copy_turned(s, j):
+            if j % 2 == 0:
+                f_stage[s, j // 2] = ring([P, 2048], BF16, "f_stage", 4, "f_stage%d_%d" % (s, j // 2))
+            words = f_stage[s, j // 2][:].bitcast(F32)[:, 512 * (j % 2) : 512 * (j % 2 + 1)]
+            nc.scalar.copy(
+                out=words.rearrange("p (g r u) -> p g r u", g=K_PASSES, u=2),
+                in_=turned[s, j][:].rearrange("p (g u r) -> p g r u", g=K_PASSES, u=2),
+            )
+
+        def quantize_f(s, h):
+            f_mx[s, h] = quantize(f_stage[s, h], E5, "f%d_%d" % (s, h))
+
+        root = {}
+        w_stage = {}
+        w_mx = {}
+
+        def inv_root(c):
+            s, h = divmod(c, CHUNKS)
+            root[c] = ring([P, PACK, CW], F32, "root", 3, "root%d" % c)
+            nc.scalar.activation(out=root[c][:], in_=v_raw[s][:, :, h * CW : (h + 1) * CW], func=ACT.Abs_reciprocal_sqrt)
+
+        def inv_square(c):
+            s, h = divmod(c, CHUNKS)
+            nc.scalar.activation(out=inv[s][:, h, :, :], in_=root[c][:], func=ACT.Square)
+
+        def staged_walk(stage, h):
+            return stage[:, h * CW * PACK : (h + 1) * CW * PACK].rearrange("p (c i t) -> p c t i", i=4, t=PACK)
+
+        def round_inv(c):
+            s, h = divmod(c, CHUNKS)
+            if h == 0:
+                w_stage[s, 0] = ring([P, 2048], BF16, "w_stage", 3, "wa_stage%d" % s)
+            nc.vector.tensor_copy(
+                out=staged_walk(w_stage[s, 0], h), in_=inv[s][:, h, :, :].rearrange("p t (c i) -> p c t i", i=4)
+            )
+
+        def round_mi(c):
+            s, h = divmod(c, CHUNKS)
+            if h == 0:
+                if s == 0:
+                    w_stage[s, 1] = ring([P, 2048], BF16, "w_stage", 3, "wb_stage%d" % s)
+                else:
+                    w_stage[s, 1] = ring([P, 2048], BF16, "x_stage", 1, "wb_stage%d" % s)
+            nc.vector.tensor_tensor(
+                out=staged_walk(w_stage[s, 1], h),
+                in0=inv[s][:, h, :, :].rearrange("p t (c i) -> p c t i", i=4),
+                in1=m_raw[s][:, :, h * CW : (h + 1) * CW].rearrange("p t (c i) -> p c t i", i=4),
+                op=ALU.mult,
+            )
+
+        def quantize_w(s, which):
+            w_mx[s, which] = quantize(w_stage[s, which], E4, "w%d_%d" % (s, which))
+
+        x_stage = {}
+        x_mx = {}
+        t_stage = {}
+        t_mx = {}
+
+        def interleave_x(s):
+            x_stage[s] = ring([P, 2048], BF16, "x_stage", 1, "x_stage%d" % s)
+            nc.gpsimd.tensor_scalar(
+                out=x_stage[s][:].rearrange("p (c t) -> p c t", t=PACK),
+                in0=x_raw[s][:].rearrange("p t c -> p c t"),
+                scalar1=1.0, scalar2=0.0, op0=ALU.mult, op1=ALU.add,
+            )
+
+        def quantize_x(s):
+            x_mx[s] = quantize(x_stage[s], E4, "x%d" % s)
+
+        def interleave_g(g, s):
+            t_stage[g, s] = ring([P, 2048], BF16, "t_stage", 4, "t_stage%d_%d" % (g, s))
+            nc.scalar.copy(
+                out=t_stage[g, s][:].rearrange("p (a m j) -> p m j a", a=PACK, j=PACK),
+                in_=g_raw[s][:, :, 512 * g : 512 * (g + 1)].rearrange("p j (m a) -> p m j a", a=PACK),
+            )
+
+        def quantize_t(g, s):
+            t_mx[g, s] = quantize(t_stage[g, s], E5, "t%d_%d" % (g, s))
+
+        steps = [(0, 0)]
+        for i in range(1, 16):
+            steps.extend([(i, 0), (i - 1, 1)])
+        steps.append((15, 1))
+        acc = {}
+        work = {}
+        state = {"pe": 0, "dve": 0}
+
+        def product(n):
+            i, which = steps[n]
+            s, j = divmod(i, PACK)
+            codes, scales = f_mx[s, j // 2]
+            acc[n] = bank(2 + n % 4, "ab%d" % n)
+            for g in range(K_PASSES):
+                cols = slice((2 * (j % 2) + g) * P, (2 * (j % 2) + g + 1) * P)
+                nc.tensor.matmul_mx(
+                    out=acc[n][:], lhsT=codes[:, cols].bitcast(E5), lhsT_scale=scales[:, cols],
+                    rhs=w_mx[g, which][0][:].bitcast(E4), rhs_scale=w_mx[g, which][1][:],
+                    start=(g == 0), stop=(g == K_PASSES - 1),
+                )
+
+        def pump():
+            while state["pe"] < len(steps) and state["pe"] < state["dve"] + 4:
+                i, which = steps[state["pe"]]
+                if (i // PACK, (i % PACK) // 2) not in f_mx or (1, which) not in w_mx:
+                    return
+                product(state["pe"])
+                state["pe"] = state["pe"] + 1
+
+        def dx_steps(count):
+            for n in range(state["dve"], state["dve"] + count):
+                i, which = steps[n]
+                s, j = divmod(i, PACK)
+                if which == 0:
+                    work[i] = ring([P, D], F32, "dx", 6, "dx%d" % i)
+                    nc.vector.tensor_tensor(out=work[i][:], in0=acc[n][:], in1=x_raw[s][:, j, :], op=ALU.mult)
+                else:
+                    nc.vector.tensor_tensor(out=work[i][:], in0=acc[n][:], in1=work[i][:], op=ALU.subtract)
+                    nc.sync.dma_start(out=dx_h[s][:, j, :], in_=work[i][:])
+                state["dve"] = n + 1
+                pump()
+
+        c_acc = {}
+        dm = {}
+        c_banks = (7, 6, 0, 1)
+
+        def product_c(i):
+            g, a = divmod(i, PACK)
+            c_acc[i] = bank(c_banks[i % 4], "c%d" % i)
+            cols = slice(a * P, (a + 1) * P)
+            for s in range(ROW_PASSES):
+                nc.tensor.matmul_mx(
+                    out=c_acc[i][:], lhsT=t_mx[g, s][0][:, cols].bitcast(E5), lhsT_scale=t_mx[g, s][1][:, cols],
+                    rhs=x_mx[s][0][:].bitcast(E4), rhs_scale=x_mx[s][1][:],
+                    start=(s == 0), stop=(s == ROW_PASSES - 1),
+                )
+
+        def dm_centre(i):
+            g, a = divmod(i, PACK)
+            dm[i] = ring([P, D], F32, "dm", 5, "dm%d" % i)
+            nc.vector.scalar_tensor_tensor(
+                out=dm[i][:], in0=m_raw[g][:, a, :], scalar=neg_g[:, g, a : a + 1], in1=c_acc[i][:],
+                op0=ALU.mult, op1=ALU.add,
+            )
+
+        def dm_scale(i, engine):
+            g, a = divmod(i, PACK)
+            view = dm[i][:].rearrange("p (h c) -> p h c", h=CHUNKS)
+            engine.tensor_tensor(out=view, in0=view, in1=inv[g][:, :, a, :], op=ALU.mult)
+            nc.sync.dma_start(out=dm_h[g][:, a, :], in_=dm[i][:])
+
+        column_sums(0)
+        for j in range(4):
+            transpose_tile(0, j, j)
+        column_sums(1)
+        transpose_tile(1, 0, 4)
+        transpose_tile(1, 1, 5)
+
+        inv_root(0)
+        for c in range(8):
+            if c + 1 < 8:
+                inv_root(c + 1)
+            inv_square(c)
+            round_inv(c)
+            if c == 4:
+                quantize_w(0, 1)
+            round_mi(c)
+            if c == 3:
+                quantize_w(0, 0)
+        quantize_w(1, 0)
+        copy_turned(0, 0)
+        copy_turned(0, 1)
+        transpose_tile(1, 2, 0)
+        transpose_tile(1, 3, 1)
+        quantize_f(0, 0)
+        copy_turned(0, 2)
+        copy_turned(0, 3)
+        quantize_f(0, 1)
+        quantize_w(1, 1)
+        interleave_x(0)
+        copy_turned(1, 0)
+        copy_turned(1, 1)
+        pump()
+        column_sums(2)
+        copy_turned(1, 2)
+        copy_turned(1, 3)
+        interleave_g(0, 0)
+        dx_steps(2)
+        transpose_tile(2, 0, 0)
+        transpose_tile(2, 1, 1)
+        dx_steps(3)
+        quantize_f(1, 0)
+        pump()
+        column_sums(3)
+        quantize_f(1, 1)
+        quantize_t(0, 0)
+        quantize_x(0)
+        interleave_x(1)
+        interleave_g(0, 1)
+        copy_sums()
+        copy_turned(2, 0)
+        copy_turned(2, 1)
+        dx_steps(3)
+        transpose_tile(2, 2, 0)
+        transpose_tile(2, 3, 1)
+        permute_sums()
+        dx_steps(2)
+        interleave_g(0, 2)
+        quantize_t(0, 1)
+        quantize_x(1)
+        interleave_x(2)
+        copy_turned(2, 2)
+        copy_turned(2, 3)
+        dx_steps(3)
+        transpose_tile(3, 0, 0)
+        transpose_tile(3, 1, 1)
+        reduce_sums()
+        dx_steps(2)
+        interleave_g(0, 3)
+        quantize_f(2, 0)
+        pump()
+        quantize_f(2, 1)
+        pump()
+        quantize_t(0, 2)
+        quantize_x(2)
+        interleave_x(3)
+        copy_turned(3, 0)
+        copy_turned(3, 1)
+        interleave_g(1, 0)
+        dx_steps(3)
+        transpose_tile(3, 2, 0)
+        transpose_tile(3, 3, 1)
+        dx_steps(2)
+        copy_turned(3, 2)
+        copy_turned(3, 3)
+        quantize_t(0, 3)
+        quantize_f(3, 0)
+        pump()
+        quantize_x(3)
+        interleave_g(1, 1)
+        product_c(0)
+        dx_steps(3)
+        product_c(1)
+        quantize_f(3, 1)
+        pump()
+        quantize_t(1, 0)
+        interleave_g(1, 2)
+        quantize_t(1, 1)
+        interleave_g(1, 3)
+        dm_centre(0)
+        dm_scale(0, nc.gpsimd)
+        dx_steps(2)
+        product_c(2)
+        quantize_t(1, 2)
+        dm_centre(1)
+        dm_scale(1, nc.gpsimd)
+        dx_steps(2)
+        product_c(3)
+        quantize_t(1, 3)
+        dm_centre(2)
+        dm_scale(2, nc.gpsimd)
+        product_c(4)
+        dx_steps(2)
+        product_c(5)
+        dm_centre(3)
+        dm_scale(3, nc.gpsimd)
+        product_c(6)
+        dx_steps(2)
+        product_c(7)
+        dm_centre(4)
+        dm_scale(4, nc.gpsimd)
+        dx_steps(1)
+        dm_centre(5)
+        dm_scale(5, nc.gpsimd)
+        dm_centre(6)
+        dm_centre(7)
+        dm_scale(6, nc.vector)
+        dm_scale(7, nc.vector)

@@ -21,7 +21,7 @@ ROW_PASSES = N // (P * PACK)
 K_PASSES = K // (P * PACK)
 CHUNKS = 4
 CW = D // CHUNKS
-SUM_N = 32
+SUM_N = 16
 
 
 def tile_gmm_pb_v_kernel(tc, x, means, vars_, grad_out, out_0, out_1):
@@ -54,8 +54,8 @@ def tile_gmm_pb_v_kernel(tc, x, means, vars_, grad_out, out_0, out_1):
         inv = [kept([P, CHUNKS, PACK, CW], F32, "inv%d" % s) for s in range(K_PASSES)]
 
         for tiles, view, s in (
-            (v_raw, v_h, 0), (m_raw, m_h, 0), (v_raw, v_h, 1), (g_raw, g_h, 0), (m_raw, m_h, 1),
-            (g_raw, g_h, 1), (x_raw, x_h, 0), (g_raw, g_h, 2), (g_raw, g_h, 3),
+            (v_raw, v_h, 0), (m_raw, m_h, 0), (g_raw, g_h, 0), (v_raw, v_h, 1), (g_raw, g_h, 1), (m_raw, m_h, 1),
+            (g_raw, g_h, 2), (x_raw, x_h, 0), (g_raw, g_h, 3),
             (x_raw, x_h, 1), (x_raw, x_h, 2), (x_raw, x_h, 3),
         ):
             nc.sync.dma_start(out=tiles[s][:], in_=view[s])
@@ -82,11 +82,11 @@ def tile_gmm_pb_v_kernel(tc, x, means, vars_, grad_out, out_0, out_1):
         sum_banks = {}
 
         def column_sums(s):
-            if s % 2 == 0:
-                sum_banks[s // 2] = bank(6 + s // 2, "sums%d" % (s // 2))
-            acc = sum_banks[s // 2]
+            if s == 0:
+                sum_banks[0] = bank(6, "sums")
+            acc = sum_banks[0]
             for b in range(8):
-                c0 = ((s % 2) * 8 + b) * SUM_N
+                c0 = (s * 8 + b) * SUM_N
                 for j in range(PACK):
                     nc.tensor.matmul(
                         acc[:, c0 : c0 + SUM_N], lhsT=g_raw[s][:, j, b * P : (b + 1) * P], rhs=ones[:],
@@ -98,8 +98,7 @@ def tile_gmm_pb_v_kernel(tc, x, means, vars_, grad_out, out_0, out_1):
         picked = {}
 
         def copy_sums():
-            for h in range(2):
-                nc.scalar.copy(out=part_sums[:, 16 * h : 16 * (h + 1)], in_=sum_banks[h][:, 0:512:SUM_N])
+            nc.scalar.copy(out=part_sums[:], in_=sum_banks[0][:, 0:512:SUM_N])
 
         def permute_sums():
             picked[0] = bank(6, "picked")
@@ -109,13 +108,12 @@ def tile_gmm_pb_v_kernel(tc, x, means, vars_, grad_out, out_0, out_1):
                     lhsT=pick[:, j, :, :].rearrange("p q m -> p (q m)"), rhs=part_sums[:], start=True, stop=True,
                 )
 
-        def reduce_sums():
+        def reduce_sums(q):
             view = picked[0][:, 0:128].rearrange("p (j s g q) -> p q g j s", j=PACK, s=ROW_PASSES, g=K_PASSES)
-            for q in range(4):
-                rows = slice(32 * q, 32 * (q + 1))
-                nc.vector.tensor_reduce(
-                    out=neg_g[rows, :, :], in_=view[rows, q, :, :, :], axis=mybir.AxisListType.X, op=ALU.add
-                )
+            rows = slice(32 * q, 32 * (q + 1))
+            nc.vector.tensor_reduce(
+                out=neg_g[rows, :, :], in_=view[rows, q, :, :, :], axis=mybir.AxisListType.X, op=ALU.add
+            )
 
         turned = {}
         f_stage = {}
@@ -147,37 +145,48 @@ def tile_gmm_pb_v_kernel(tc, x, means, vars_, grad_out, out_0, out_1):
         w_stage = {}
         w_mx = {}
 
+        pieces = [(0, 0, 0, 64), (0, 0, 64, CW)] + [(c // CHUNKS, c % CHUNKS, 0, CW) for c in range(1, 8)]
+
         def inv_root(c):
-            s, h = divmod(c, CHUNKS)
-            root[c] = ring([P, PACK, CW], F32, "root", 3, "root%d" % c)
-            nc.scalar.activation(out=root[c][:], in_=v_raw[s][:, :, h * CW : (h + 1) * CW], func=ACT.Abs_reciprocal_sqrt)
+            s, h, c0, c1 = pieces[c]
+            root[c] = ring([P, PACK, c1 - c0], F32, "root", 4, "root%d" % c)
+            nc.scalar.activation(
+                out=root[c][:], in_=v_raw[s][:, :, h * CW + c0 : h * CW + c1], func=ACT.Abs_reciprocal_sqrt
+            )
 
         def inv_square(c):
-            s, h = divmod(c, CHUNKS)
-            nc.scalar.activation(out=inv[s][:, h, :, :], in_=root[c][:], func=ACT.Square)
+            s, h, c0, c1 = pieces[c]
+            nc.scalar.activation(out=inv[s][:, h, :, c0:c1], in_=root[c][:], func=ACT.Square)
 
-        def staged_walk(stage, h):
-            return stage[:, h * CW * PACK : (h + 1) * CW * PACK].rearrange("p (c i t) -> p c t i", i=4, t=PACK)
+        def staged_walk(s, which, h, c0, c1):
+            if (s, which) not in w_stage:
+                if (s, which) == (1, 1):
+                    w_stage[s, which] = ring([P, 2048], BF16, "x_stage", 1, "w_stage%d_%d" % (s, which))
+                else:
+                    w_stage[s, which] = ring([P, 2048], BF16, "w_stage", 3, "w_stage%d_%d" % (s, which))
+            cols = slice((h * CW + c0) * PACK, (h * CW + c1) * PACK)
+            return w_stage[s, which][:, cols].rearrange("p (c i t) -> p c t i", i=4, t=PACK)
 
         def round_inv(c):
-            s, h = divmod(c, CHUNKS)
-            if h == 0:
-                w_stage[s, 0] = ring([P, 2048], BF16, "w_stage", 3, "wa_stage%d" % s)
+            s, h, c0, c1 = pieces[c]
             nc.vector.tensor_copy(
-                out=staged_walk(w_stage[s, 0], h), in_=inv[s][:, h, :, :].rearrange("p t (c i) -> p c t i", i=4)
+                out=staged_walk(s, 0, h, c0, c1),
+                in_=inv[s][:, h, :, c0:c1].rearrange("p t (c i) -> p c t i", i=4),
+            )
+
+        def round_inv_scalar(c):
+            s, h, c0, c1 = pieces[c]
+            nc.scalar.activation(
+                out=staged_walk(s, 0, h, c0, c1),
+                in_=root[c][:].rearrange("p t (c i) -> p c t i", i=4), func=ACT.Square,
             )
 
         def round_mi(c):
-            s, h = divmod(c, CHUNKS)
-            if h == 0:
-                if s == 0:
-                    w_stage[s, 1] = ring([P, 2048], BF16, "w_stage", 3, "wb_stage%d" % s)
-                else:
-                    w_stage[s, 1] = ring([P, 2048], BF16, "x_stage", 1, "wb_stage%d" % s)
+            s, h, c0, c1 = pieces[c]
             nc.vector.tensor_tensor(
-                out=staged_walk(w_stage[s, 1], h),
-                in0=inv[s][:, h, :, :].rearrange("p t (c i) -> p c t i", i=4),
-                in1=m_raw[s][:, :, h * CW : (h + 1) * CW].rearrange("p t (c i) -> p c t i", i=4),
+                out=staged_walk(s, 1, h, c0, c1),
+                in0=inv[s][:, h, :, c0:c1].rearrange("p t (c i) -> p c t i", i=4),
+                in1=m_raw[s][:, :, h * CW + c0 : h * CW + c1].rearrange("p t (c i) -> p c t i", i=4),
                 op=ALU.mult,
             )
 
@@ -231,15 +240,15 @@ def tile_gmm_pb_v_kernel(tc, x, means, vars_, grad_out, out_0, out_1):
                     start=(g == 0), stop=(g == K_PASSES - 1),
                 )
 
-        def pump():
-            while state["pe"] < len(steps) and state["pe"] < state["dve"] + 4:
+        def pump(most=32):
+            while state["pe"] < most and state["pe"] < state["dve"] + 4:
                 i, which = steps[state["pe"]]
                 if (i // PACK, (i % PACK) // 2) not in f_mx or (1, which) not in w_mx:
                     return
                 product(state["pe"])
                 state["pe"] = state["pe"] + 1
 
-        def dx_steps(count):
+        def dx_steps(count, most=32):
             for n in range(state["dve"], state["dve"] + count):
                 i, which = steps[n]
                 s, j = divmod(i, PACK)
@@ -250,17 +259,18 @@ def tile_gmm_pb_v_kernel(tc, x, means, vars_, grad_out, out_0, out_1):
                     nc.vector.tensor_tensor(out=work[i][:], in0=acc[n][:], in1=work[i][:], op=ALU.subtract)
                     nc.sync.dma_start(out=dx_h[s][:, j, :], in_=work[i][:])
                 state["dve"] = n + 1
-                pump()
+                pump(most)
 
         c_acc = {}
         dm = {}
-        c_banks = (7, 6, 0, 1)
+        c_banks = (0, 6, 1, 7, 0, 6, 1, 7)
 
-        def product_c(i):
+        def product_c(i, passes=range(ROW_PASSES)):
             g, a = divmod(i, PACK)
-            c_acc[i] = bank(c_banks[i % 4], "c%d" % i)
+            if i not in c_acc:
+                c_acc[i] = bank(c_banks[i], "c%d" % i)
             cols = slice(a * P, (a + 1) * P)
-            for s in range(ROW_PASSES):
+            for s in passes:
                 nc.tensor.matmul_mx(
                     out=c_acc[i][:], lhsT=t_mx[g, s][0][:, cols].bitcast(E5), lhsT_scale=t_mx[g, s][1][:, cols],
                     rhs=x_mx[s][0][:].bitcast(E4), rhs_scale=x_mx[s][1][:],
@@ -269,7 +279,7 @@ def tile_gmm_pb_v_kernel(tc, x, means, vars_, grad_out, out_0, out_1):
 
         def dm_centre(i):
             g, a = divmod(i, PACK)
-            dm[i] = ring([P, D], F32, "dm", 5, "dm%d" % i)
+            dm[i] = ring([P, D], F32, "dm", 6, "dm%d" % i)
             nc.vector.scalar_tensor_tensor(
                 out=dm[i][:], in0=m_raw[g][:, a, :], scalar=neg_g[:, g, a : a + 1], in1=c_acc[i][:],
                 op0=ALU.mult, op1=ALU.add,
@@ -287,124 +297,143 @@ def tile_gmm_pb_v_kernel(tc, x, means, vars_, grad_out, out_0, out_1):
         column_sums(1)
         transpose_tile(1, 0, 4)
         transpose_tile(1, 1, 5)
-
+        transpose_tile(1, 2, 7)
+        column_sums(2)
         inv_root(0)
-        for c in range(8):
-            if c + 1 < 8:
+        for c in range(5):
+            if c < 4:
                 inv_root(c + 1)
             inv_square(c)
             round_inv(c)
-            if c == 4:
-                quantize_w(0, 1)
             round_mi(c)
-            if c == 3:
-                quantize_w(0, 0)
-        quantize_w(1, 0)
+        inv_root(5)
+        quantize_w(0, 0)
+        inv_root(6)
+        inv_square(5)
+        round_inv(5)
+        quantize_w(0, 1)
+        inv_root(7)
+        inv_square(6)
+        round_inv(6)
+        round_mi(5)
+        inv_root(8)
+        inv_square(7)
+        inv_square(8)
+        round_inv_scalar(7)
+        round_inv_scalar(8)
+        round_mi(6)
+        round_mi(7)
         copy_turned(0, 0)
+        transpose_tile(1, 3, 0)
         copy_turned(0, 1)
-        transpose_tile(1, 2, 0)
-        transpose_tile(1, 3, 1)
+        transpose_tile(2, 0, 1)
+        quantize_w(1, 0)
+        round_mi(8)
         quantize_f(0, 0)
         copy_turned(0, 2)
         copy_turned(0, 3)
+        pump()
         quantize_f(0, 1)
         quantize_w(1, 1)
         interleave_x(0)
         copy_turned(1, 0)
         copy_turned(1, 1)
         pump()
-        column_sums(2)
         copy_turned(1, 2)
         copy_turned(1, 3)
         interleave_g(0, 0)
-        dx_steps(2)
-        transpose_tile(2, 0, 0)
-        transpose_tile(2, 1, 1)
         dx_steps(3)
+        transpose_tile(2, 1, 7)
+        transpose_tile(2, 2, 0)
+        dx_steps(2)
         quantize_f(1, 0)
+        copy_turned(2, 0)
+        transpose_tile(2, 3, 1)
         pump()
-        column_sums(3)
         quantize_f(1, 1)
         quantize_t(0, 0)
         quantize_x(0)
         interleave_x(1)
         interleave_g(0, 1)
-        copy_sums()
-        copy_turned(2, 0)
         copy_turned(2, 1)
-        dx_steps(3)
-        transpose_tile(2, 2, 0)
-        transpose_tile(2, 3, 1)
-        permute_sums()
-        dx_steps(2)
-        interleave_g(0, 2)
-        quantize_t(0, 1)
-        quantize_x(1)
-        interleave_x(2)
         copy_turned(2, 2)
         copy_turned(2, 3)
-        dx_steps(3)
-        transpose_tile(3, 0, 0)
-        transpose_tile(3, 1, 1)
-        reduce_sums()
-        dx_steps(2)
-        interleave_g(0, 3)
+        dx_steps(5)
+        column_sums(3)
+        transpose_tile(3, 0, 7)
+        transpose_tile(3, 1, 0)
+        interleave_g(0, 2)
+        copy_sums()
+        quantize_t(0, 1)
         quantize_f(2, 0)
-        pump()
+        quantize_x(1)
+        interleave_x(2)
+        copy_turned(3, 0)
+        copy_turned(3, 1)
+        interleave_g(0, 3)
+        dx_steps(5)
+        permute_sums()
+        transpose_tile(3, 2, 1)
+        transpose_tile(3, 3, 7)
         quantize_f(2, 1)
         pump()
         quantize_t(0, 2)
         quantize_x(2)
         interleave_x(3)
-        copy_turned(3, 0)
-        copy_turned(3, 1)
         interleave_g(1, 0)
-        dx_steps(3)
-        transpose_tile(3, 2, 0)
-        transpose_tile(3, 3, 1)
-        dx_steps(2)
+        dx_steps(1)
+        for q in range(4):
+            reduce_sums(q)
+            dx_steps(1)
+        product_c(0, range(3))
+        quantize_t(0, 3)
+        quantize_x(3)
+        product_c(0, range(3, 4))
+        product_c(1)
         copy_turned(3, 2)
         copy_turned(3, 3)
-        quantize_t(0, 3)
-        quantize_f(3, 0)
-        pump()
-        quantize_x(3)
         interleave_g(1, 1)
-        product_c(0)
-        dx_steps(3)
-        product_c(1)
-        quantize_f(3, 1)
+        dx_steps(1)
+        dm_centre(0)
+        product_c(2)
+        product_c(3)
+        dx_steps(2)
+        dm_scale(0, nc.gpsimd)
+        quantize_f(3, 0)
         pump()
         quantize_t(1, 0)
         interleave_g(1, 2)
+        quantize_f(3, 1)
         quantize_t(1, 1)
         interleave_g(1, 3)
-        dm_centre(0)
-        dm_scale(0, nc.gpsimd)
-        dx_steps(2)
-        product_c(2)
-        quantize_t(1, 2)
         dm_centre(1)
-        dm_scale(1, nc.gpsimd)
-        dx_steps(2)
-        product_c(3)
-        quantize_t(1, 3)
         dm_centre(2)
-        dm_scale(2, nc.gpsimd)
-        product_c(4)
-        dx_steps(2)
-        product_c(5)
         dm_centre(3)
-        dm_scale(3, nc.gpsimd)
-        product_c(6)
+        dm_scale(1, nc.gpsimd)
+        product_c(4, range(2))
+        product_c(5, range(2))
         dx_steps(2)
-        product_c(7)
+        dm_scale(2, nc.gpsimd)
+        product_c(6, range(2))
+        product_c(7, range(2))
+        dx_steps(2, 29)
+        dm_scale(3, nc.gpsimd)
+        quantize_t(1, 2)
+        quantize_t(1, 3)
+        product_c(4, range(2, 4))
+        product_c(5, range(2, 4))
+        dx_steps(1, 30)
         dm_centre(4)
-        dm_scale(4, nc.gpsimd)
-        dx_steps(1)
+        pump()
         dm_centre(5)
+        dx_steps(1, 31)
+        dm_scale(4, nc.gpsimd)
+        product_c(6, range(2, 4))
+        dx_steps(2)
         dm_scale(5, nc.gpsimd)
+        product_c(7, range(2, 4))
         dm_centre(6)
+        dx_steps(1)
+        dm_scale(6, nc.gpsimd)
         dm_centre(7)
-        dm_scale(6, nc.vector)
         dm_scale(7, nc.vector)

@@ -21,7 +21,6 @@ ROW_PASSES = N // (P * PACK)
 K_PASSES = K // (P * PACK)
 CHUNKS = 4
 CW = D // CHUNKS
-SUM_N = 16
 
 
 def tile_gmm_pb_v_kernel(tc, x, means, vars_, grad_out, out_0, out_1):
@@ -61,17 +60,13 @@ def tile_gmm_pb_v_kernel(tc, x, means, vars_, grad_out, out_0, out_1):
             nc.sync.dma_start(out=tiles[s][:], in_=view[s])
 
         ident = kept([P, P], F32, "ident")
-        ones_f = kept([P, SUM_N], F32, "ones_f")
-        ones = kept([P, SUM_N], BF16, "ones")
-        pick = kept([P, PACK, 4, 32], F32, "pick")
-        nc.vector.memset(ones_f[:], 1.0)
-        nc.scalar.activation(out=ones[:], in_=ones_f[:], func=ACT.Abs_reciprocal_sqrt)
+        quarter = kept([P, 64], F32, "quarter")
+        halves = kept([P, K_PASSES, P], BF16, "halves")
+        nc.vector.memset(quarter[:], 1.0)
+        nc.vector.memset(halves[:], 0.0)
+        for g in range(K_PASSES):
+            nc.scalar.activation(out=halves[:, g, 64 * g : 64 * (g + 1)], in_=quarter[:], func=ACT.Abs_reciprocal_sqrt)
         make_identity(nc, ident[:])
-        for q in range(4):
-            nc.vector.tensor_scalar(
-                out=pick[:, :, q, :], in0=ident[:].rearrange("p (m j) -> p j m", j=PACK),
-                scalar1=-1.0, scalar2=None, op0=ALU.mult,
-            )
 
         def quantize(staged, fmt, name):
             codes = kept([P, 512], U32, name + "_codes")
@@ -79,50 +74,44 @@ def tile_gmm_pb_v_kernel(tc, x, means, vars_, grad_out, out_0, out_1):
             nc.vector.quantize_mx(out=codes[:].bitcast(fmt), scales=scales[:], in_=staged[:])
             return codes, scales
 
-        sum_banks = {}
-
-        def column_sums(s):
-            if s == 0:
-                sum_banks[0] = bank(6, "sums")
-            acc = sum_banks[0]
-            for b in range(8):
-                c0 = (s * 8 + b) * SUM_N
-                for j in range(PACK):
-                    nc.tensor.matmul(
-                        acc[:, c0 : c0 + SUM_N], lhsT=g_raw[s][:, j, b * P : (b + 1) * P], rhs=ones[:],
-                        start=(j == 0), stop=(j == PACK - 1),
-                    )
-
-        part_sums = kept([P, 32], F32, "part_sums")
-        neg_g = kept([P, K_PASSES, PACK], F32, "neg_g")
+        sums = bank(6, "sums")
+        sum_rows = kept([P, PACK, P], F32, "sum_rows")
+        neg_g = kept([P, PACK, K_PASSES], F32, "neg_g")
         picked = {}
 
-        def copy_sums():
-            nc.scalar.copy(out=part_sums[:], in_=sum_banks[0][:, 0:512:SUM_N])
-
-        def permute_sums():
-            picked[0] = bank(6, "picked")
-            for j in range(PACK):
-                nc.tensor.matmul(
-                    picked[0][:, 32 * j : 32 * (j + 1)],
-                    lhsT=pick[:, j, :, :].rearrange("p q m -> p (q m)"), rhs=part_sums[:], start=True, stop=True,
-                )
-
-        def reduce_sums(q):
-            view = picked[0][:, 0:128].rearrange("p (j s g q) -> p q g j s", j=PACK, s=ROW_PASSES, g=K_PASSES)
-            rows = slice(32 * q, 32 * (q + 1))
-            nc.vector.tensor_reduce(
-                out=neg_g[rows, :, :], in_=view[rows, q, :, :, :], axis=mybir.AxisListType.X, op=ALU.add
+        def column_sum(s, j, g):
+            nc.tensor.matmul(
+                sums[:], lhsT=halves[:, g, :], rhs=g_raw[s][:, j, 512 * g : 512 * (g + 1)],
+                start=(s == 0 and j == 0 and g == 0), stop=(s == ROW_PASSES - 1 and j == PACK - 1 and g == 1),
             )
+
+        def column_sums(s, j):
+            for g in range(K_PASSES):
+                column_sum(s, j, g)
+
+        def copy_sums():
+            nc.scalar.activation(
+                out=sum_rows[:], in_=sums[:].rearrange("p (m a) -> p a m", a=PACK), func=ACT.Copy, scale=-1.0
+            )
+
+        def turn_sums():
+            picked[0] = bank(6, "picked")
+            for a in range(PACK):
+                nc.tensor.transpose(picked[0][:, a * P : (a + 1) * P], sum_rows[:, a, :], ident[:])
+
+        def pick_sums():
+            nc.scalar.copy(out=neg_g[:].rearrange("p a g -> p (a g)"), in_=picked[0][:, 0:512:64])
 
         turned = {}
         f_stage = {}
         f_mx = {}
 
-        def transpose_tile(s, j, b):
+        def transpose_tile(s, j, b, sums_of=None):
             turned[s, j] = bank(b, "turned%d_%d" % (s, j))
             words = g_raw[s][:, j, :].bitcast(F32)
             for g in range(K_PASSES):
+                if sums_of is not None:
+                    column_sum(sums_of[0], sums_of[1], g)
                 for u in range(2):
                     c0 = (2 * g + u) * P
                     nc.tensor.transpose(
@@ -281,7 +270,7 @@ def tile_gmm_pb_v_kernel(tc, x, means, vars_, grad_out, out_0, out_1):
             g, a = divmod(i, PACK)
             dm[i] = ring([P, D], F32, "dm", 6, "dm%d" % i)
             nc.vector.scalar_tensor_tensor(
-                out=dm[i][:], in0=m_raw[g][:, a, :], scalar=neg_g[:, g, a : a + 1], in1=c_acc[i][:],
+                out=dm[i][:], in0=m_raw[g][:, a, :], scalar=neg_g[:, a, g : g + 1], in1=c_acc[i][:],
                 op0=ALU.mult, op1=ALU.add,
             )
 
@@ -291,14 +280,14 @@ def tile_gmm_pb_v_kernel(tc, x, means, vars_, grad_out, out_0, out_1):
             engine.tensor_tensor(out=view, in0=view, in1=inv[g][:, :, a, :], op=ALU.mult)
             nc.sync.dma_start(out=dm_h[g][:, a, :], in_=dm[i][:])
 
-        column_sums(0)
-        for j in range(4):
-            transpose_tile(0, j, j)
-        column_sums(1)
-        transpose_tile(1, 0, 4)
-        transpose_tile(1, 1, 5)
-        transpose_tile(1, 2, 7)
-        column_sums(2)
+        column_sums(0, 0)
+        for j in range(3):
+            transpose_tile(0, j, j, (0, j + 1))
+        transpose_tile(0, 3, 3)
+        transpose_tile(1, 0, 4, (1, 0))
+        transpose_tile(1, 1, 5, (1, 1))
+        transpose_tile(1, 2, 7, (1, 2))
+        column_sums(2, 0)
         inv_root(0)
         for c in range(5):
             if c < 4:
@@ -324,9 +313,9 @@ def tile_gmm_pb_v_kernel(tc, x, means, vars_, grad_out, out_0, out_1):
         round_mi(6)
         round_mi(7)
         copy_turned(0, 0)
-        transpose_tile(1, 3, 0)
+        transpose_tile(1, 3, 0, (1, 3))
         copy_turned(0, 1)
-        transpose_tile(2, 0, 1)
+        transpose_tile(2, 0, 1, (2, 1))
         quantize_w(1, 0)
         round_mi(8)
         quantize_f(0, 0)
@@ -343,12 +332,12 @@ def tile_gmm_pb_v_kernel(tc, x, means, vars_, grad_out, out_0, out_1):
         copy_turned(1, 3)
         interleave_g(0, 0)
         dx_steps(3)
-        transpose_tile(2, 1, 7)
-        transpose_tile(2, 2, 0)
+        transpose_tile(2, 1, 7, (2, 2))
+        transpose_tile(2, 2, 0, (2, 3))
         dx_steps(2)
         quantize_f(1, 0)
         copy_turned(2, 0)
-        transpose_tile(2, 3, 1)
+        transpose_tile(2, 3, 1, (3, 0))
         pump()
         quantize_f(1, 1)
         quantize_t(0, 0)
@@ -359,20 +348,20 @@ def tile_gmm_pb_v_kernel(tc, x, means, vars_, grad_out, out_0, out_1):
         copy_turned(2, 2)
         copy_turned(2, 3)
         dx_steps(5)
-        column_sums(3)
-        transpose_tile(3, 0, 7)
-        transpose_tile(3, 1, 0)
+        transpose_tile(3, 0, 7, (3, 1))
+        transpose_tile(3, 1, 0, (3, 2))
+        column_sums(3, 3)
         interleave_g(0, 2)
-        copy_sums()
         quantize_t(0, 1)
         quantize_f(2, 0)
         quantize_x(1)
         interleave_x(2)
         copy_turned(3, 0)
         copy_turned(3, 1)
+        copy_sums()
         interleave_g(0, 3)
         dx_steps(5)
-        permute_sums()
+        turn_sums()
         transpose_tile(3, 2, 1)
         transpose_tile(3, 3, 7)
         quantize_f(2, 1)
@@ -380,11 +369,9 @@ def tile_gmm_pb_v_kernel(tc, x, means, vars_, grad_out, out_0, out_1):
         quantize_t(0, 2)
         quantize_x(2)
         interleave_x(3)
+        pick_sums()
         interleave_g(1, 0)
-        dx_steps(1)
-        for q in range(4):
-            reduce_sums(q)
-            dx_steps(1)
+        dx_steps(5)
         product_c(0, range(3))
         quantize_t(0, 3)
         quantize_x(3)

from contextlib import ExitStack

import concourse.mybir as mybir
from concourse.masks import make_identity

N, D, K = 2048, 512, 1024
FLOPS = 2 * N * K * 2 * D + 2 * K * N * D

F32 = mybir.dt.float32
BF16 = mybir.dt.bfloat16
U32 = mybir.dt.uint32
U8 = mybir.dt.uint8
E4 = mybir.dt.float8_e4m3fn_x4
E5 = mybir.dt.float8_e5m2_x4
ALU = mybir.AluOpType
ACT = mybir.ActivationFunctionType

P = 128
PACK = 4
ROW_PASSES = N // (P * PACK)
K_PASSES = K // (P * PACK)
CHUNKS = 4
CW = D // CHUNKS


def tile_gmm_pb_v_kernel(tc, x, means, vars_, grad_out, out_0, out_1):
    nc = tc.nc
    x_h = x.rearrange("(s p j) d -> s p j d", p=P, j=PACK)
    g_h = grad_out.rearrange("(s p j) k -> s p j k", p=P, j=PACK)
    m_h = means.rearrange("(s p j) d -> s p j d", p=P, j=PACK)
    v_h = vars_.rearrange("(s p j) d -> s p j d", p=P, j=PACK)
    dx_h = out_0.rearrange("(s p j) d -> s p j d", p=P, j=PACK)
    dm_h = out_1.rearrange("(s p j) d -> s p j d", p=P, j=PACK)

    with ExitStack() as ctx:
        keep = ctx.enter_context(tc.tile_pool(name="keep", bufs=1))
        psum = ctx.enter_context(tc.psum_pool(name="psum", bufs=1))
        ctx.enter_context(tc.manual_schedule())

        def bank(b, name):
            return psum.tile([P, 512], F32, tag="bank%d" % b, name=name)

        def kept(shape, dtype, name):
            return keep.tile(shape, dtype, name=name, align_bytes=64)

        def ring(shape, dtype, tag, bufs, name):
            return keep.tile(shape, dtype, tag=tag, bufs=bufs, name=name, align_bytes=64)

        v_raw = [kept([P, PACK, D], BF16, "v_raw%d" % s) for s in range(K_PASSES)]
        m_raw = [kept([P, PACK, D], BF16, "m_raw%d" % s) for s in range(K_PASSES)]
        g_raw = [kept([P, PACK, K], BF16, "g_raw%d" % s) for s in range(ROW_PASSES)]
        x_raw = [kept([P, PACK, D], BF16, "x_raw%d" % s) for s in range(ROW_PASSES)]
        inv = [kept([P, CHUNKS, PACK, CW], F32, "inv%d" % s) for s in range(K_PASSES)]

        for tiles, view, s in (
            (v_raw, v_h, 0), (m_raw, m_h, 0), (g_raw, g_h, 0), (v_raw, v_h, 1), (g_raw, g_h, 1), (m_raw, m_h, 1),
            (g_raw, g_h, 2), (x_raw, x_h, 0), (g_raw, g_h, 3),
            (x_raw, x_h, 1), (x_raw, x_h, 2), (x_raw, x_h, 3),
        ):
            nc.sync.dma_start(out=tiles[s][:], in_=view[s])

        ident = kept([P, P], F32, "ident")
        quarter = kept([P, 64], F32, "quarter")
        halves = kept([P, K_PASSES, P], BF16, "halves")
        nc.vector.memset(quarter[:], 1.0)
        nc.vector.memset(halves[:], 0.0)
        for g in range(K_PASSES):
            nc.scalar.activation(out=halves[:, g, 64 * g : 64 * (g + 1)], in_=quarter[:], func=ACT.Abs_reciprocal_sqrt)
        make_identity(nc, ident[:])

        def quantize(staged, fmt, name):
            codes = kept([P, 512], U32, name + "_codes")
            scales = kept([P, 512], U8, name + "_scales")
            nc.vector.quantize_mx(out=codes[:].bitcast(fmt), scales=scales[:], in_=staged[:])
            return codes, scales

        sums = bank(6, "sums")
        sum_rows = kept([P, PACK, P], F32, "sum_rows")
        neg_g = kept([P, PACK, K_PASSES], F32, "neg_g")
        picked = {}

        def column_sum(s, j, g):
            nc.tensor.matmul(
                sums[:], lhsT=halves[:, g, :], rhs=g_raw[s][:, j, 512 * g : 512 * (g + 1)],
                start=(s == 0 and j == 0 and g == 0), stop=(s == ROW_PASSES - 1 and j == PACK - 1 and g == 1),
            )

        def column_sums(s, j):
            for g in range(K_PASSES):
                column_sum(s, j, g)

        def copy_sums():
            nc.scalar.activation(
                out=sum_rows[:], in_=sums[:].rearrange("p (m a) -> p a m", a=PACK), func=ACT.Copy, scale=-1.0
            )

        def turn_sums():
            picked[0] = bank(6, "picked")
            for a in range(PACK):
                nc.tensor.transpose(picked[0][:, a * P : (a + 1) * P], sum_rows[:, a, :], ident[:])

        def pick_sums():
            nc.scalar.copy(out=neg_g[:].rearrange("p a g -> p (a g)"), in_=picked[0][:, 0:512:64])

        turned = {}
        f_stage = {}
        f_mx = {}

        def transpose_tile(s, j, b, sums_of=None):
            turned[s, j] = bank(b, "turned%d_%d" % (s, j))
            words = g_raw[s][:, j, :].bitcast(F32)
            for g in range(K_PASSES):
                if sums_of is not None:
                    column_sum(sums_of[0], sums_of[1], g)
                for u in range(2):
                    c0 = (2 * g + u) * P
                    nc.tensor.transpose(
                        turned[s, j][:, c0 : c0 + P], words[:, 256 * g + u : 256 * (g + 1) : 2], ident[:]
                    )

        def copy_turned(s, j):
            if j % 2 == 0:
                f_stage[s, j // 2] = ring([P, 2048], BF16, "f_stage", 4, "f_stage%d_%d" % (s, j // 2))
            words = f_stage[s, j // 2][:].bitcast(F32)[:, 512 * (j % 2) : 512 * (j % 2 + 1)]
            nc.scalar.copy(
                out=words.rearrange("p (g r u) -> p g r u", g=K_PASSES, u=2),
                in_=turned[s, j][:].rearrange("p (g u r) -> p g r u", g=K_PASSES, u=2),
            )

        def quantize_f(s, h):
            f_mx[s, h] = quantize(f_stage[s, h], E5, "f%d_%d" % (s, h))

        root = {}
        w_stage = {}
        w_mx = {}

        pieces = [(0, 0, 0, 64), (0, 0, 64, CW)] + [(c // CHUNKS, c % CHUNKS, 0, CW) for c in range(1, 8)]

        def inv_root(c):
            s, h, c0, c1 = pieces[c]
            root[c] = ring([P, PACK, c1 - c0], F32, "root", 4, "root%d" % c)
            nc.scalar.activation(
                out=root[c][:], in_=v_raw[s][:, :, h * CW + c0 : h * CW + c1], func=ACT.Abs_reciprocal_sqrt
            )

        def inv_square(c):
            s, h, c0, c1 = pieces[c]
            nc.scalar.activation(out=inv[s][:, h, :, c0:c1], in_=root[c][:], func=ACT.Square)

        def staged_walk(s, which, h, c0, c1):
            if (s, which) not in w_stage:
                if (s, which) == (1, 1):
                    w_stage[s, which] = ring([P, 2048], BF16, "x_stage", 1, "w_stage%d_%d" % (s, which))
                else:
                    w_stage[s, which] = ring([P, 2048], BF16, "w_stage", 3, "w_stage%d_%d" % (s, which))
            cols = slice((h * CW + c0) * PACK, (h * CW + c1) * PACK)
            return w_stage[s, which][:, cols].rearrange("p (c i t) -> p c t i", i=4, t=PACK)

        def round_inv(c):
            s, h, c0, c1 = pieces[c]
            nc.vector.tensor_copy(
                out=staged_walk(s, 0, h, c0, c1),
                in_=inv[s][:, h, :, c0:c1].rearrange("p t (c i) -> p c t i", i=4),
            )

        def round_inv_scalar(c):
            s, h, c0, c1 = pieces[c]
            nc.scalar.activation(
                out=staged_walk(s, 0, h, c0, c1),
                in_=root[c][:].rearrange("p t (c i) -> p c t i", i=4), func=ACT.Square,
            )

        def round_mi(c):
            s, h, c0, c1 = pieces[c]
            nc.vector.tensor_tensor(
                out=staged_walk(s, 1, h, c0, c1),
                in0=inv[s][:, h, :, c0:c1].rearrange("p t (c i) -> p c t i", i=4),
                in1=m_raw[s][:, :, h * CW + c0 : h * CW + c1].rearrange("p t (c i) -> p c t i", i=4),
                op=ALU.mult,
            )

        def quantize_w(s, which):
            w_mx[s, which] = quantize(w_stage[s, which], E4, "w%d_%d" % (s, which))

        x_stage = {}
        x_mx = {}
        t_stage = {}
        t_mx = {}

        def interleave_x(s):
            x_stage[s] = ring([P, 2048], BF16, "x_stage", 1, "x_stage%d" % s)
            nc.gpsimd.tensor_scalar(
                out=x_stage[s][:].rearrange("p (c t) -> p c t", t=PACK),
                in0=x_raw[s][:].rearrange("p t c -> p c t"),
                scalar1=1.0, scalar2=0.0, op0=ALU.mult, op1=ALU.add,
            )

        def quantize_x(s):
            x_mx[s] = quantize(x_stage[s], E4, "x%d" % s)

        def interleave_g(g, s):
            t_stage[g, s] = ring([P, 2048], BF16, "t_stage", 4, "t_stage%d_%d" % (g, s))
            nc.scalar.copy(
                out=t_stage[g, s][:].rearrange("p (a m j) -> p m j a", a=PACK, j=PACK),
                in_=g_raw[s][:, :, 512 * g : 512 * (g + 1)].rearrange("p j (m a) -> p m j a", a=PACK),
            )

        def quantize_t(g, s):
            t_mx[g, s] = quantize(t_stage[g, s], E5, "t%d_%d" % (g, s))

        steps = [(0, 0)]
        for i in range(1, 16):
            steps.extend([(i, 0), (i - 1, 1)])
        steps.append((15, 1))
        acc = {}
        work = {}
        state = {"pe": 0, "dve": 0}

        def product(n):
            i, which = steps[n]
            s, j = divmod(i, PACK)
            codes, scales = f_mx[s, j // 2]
            acc[n] = bank(2 + n % 4, "ab%d" % n)
            for g in range(K_PASSES):
                cols = slice((2 * (j % 2) + g) * P, (2 * (j % 2) + g + 1) * P)
                nc.tensor.matmul_mx(
                    out=acc[n][:], lhsT=codes[:, cols].bitcast(E5), lhsT_scale=scales[:, cols],
                    rhs=w_mx[g, which][0][:].bitcast(E4), rhs_scale=w_mx[g, which][1][:],
                    start=(g == 0), stop=(g == K_PASSES - 1),
                )

        def pump(most=32):
            while state["pe"] < most and state["pe"] < state["dve"] + 4:
                i, which = steps[state["pe"]]
                if (i // PACK, (i % PACK) // 2) not in f_mx or (1, which) not in w_mx:
                    return
                product(state["pe"])
                state["pe"] = state["pe"] + 1

        def dx_steps(count, most=32):
            for n in range(state["dve"], state["dve"] + count):
                i, which = steps[n]
                s, j = divmod(i, PACK)
                if which == 0:
                    work[i] = ring([P, D], F32, "dx", 6, "dx%d" % i)
                    nc.vector.tensor_tensor(out=work[i][:], in0=acc[n][:], in1=x_raw[s][:, j, :], op=ALU.mult)
                else:
                    nc.vector.tensor_tensor(out=work[i][:], in0=acc[n][:], in1=work[i][:], op=ALU.subtract)
                    nc.sync.dma_start(out=dx_h[s][:, j, :], in_=work[i][:])
                state["dve"] = n + 1
                pump(most)

        c_acc = {}
        dm = {}
        c_banks = (0, 6, 1, 7, 0, 6, 1, 7)

        def product_c(i, passes=range(ROW_PASSES)):
            g, a = divmod(i, PACK)
            if i not in c_acc:
                c_acc[i] = bank(c_banks[i], "c%d" % i)
            cols = slice(a * P, (a + 1) * P)
            for s in passes:
                nc.tensor.matmul_mx(
                    out=c_acc[i][:], lhsT=t_mx[g, s][0][:, cols].bitcast(E5), lhsT_scale=t_mx[g, s][1][:, cols],
                    rhs=x_mx[s][0][:].bitcast(E4), rhs_scale=x_mx[s][1][:],
                    start=(s == 0), stop=(s == ROW_PASSES - 1),
                )

        def dm_centre(i):
            g, a = divmod(i, PACK)
            dm[i] = ring([P, D], F32, "dm", 6, "dm%d" % i)
            nc.vector.scalar_tensor_tensor(
                out=dm[i][:], in0=m_raw[g][:, a, :], scalar=neg_g[:, a, g : g + 1], in1=c_acc[i][:],
                op0=ALU.mult, op1=ALU.add,
            )

        def dm_scale(i, engine):
            g, a = divmod(i, PACK)
            view = dm[i][:].rearrange("p (h c) -> p h c", h=CHUNKS)
            engine.tensor_tensor(out=view, in0=view, in1=inv[g][:, :, a, :], op=ALU.mult)
            nc.sync.dma_start(out=dm_h[g][:, a, :], in_=dm[i][:])

        column_sums(0, 0)
        for j in range(3):
            transpose_tile(0, j, j, (0, j + 1))
        transpose_tile(0, 3, 3)
        transpose_tile(1, 0, 4, (1, 0))
        transpose_tile(1, 1, 5, (1, 1))
        transpose_tile(1, 2, 7, (1, 2))
        column_sums(2, 0)
        inv_root(0)
        for c in range(5):
            if c < 4:
                inv_root(c + 1)
            inv_square(c)
            round_inv(c)
            round_mi(c)
        inv_root(5)
        quantize_w(0, 0)
        inv_root(6)
        inv_square(5)
        round_inv(5)
        quantize_w(0, 1)
        inv_root(7)
        inv_square(6)
        round_inv(6)
        round_mi(5)
        inv_root(8)
        inv_square(7)
        inv_square(8)
        round_inv_scalar(7)
        round_inv_scalar(8)
        round_mi(6)
        round_mi(7)
        copy_turned(0, 0)
        transpose_tile(1, 3, 0, (1, 3))
        copy_turned(0, 1)
        transpose_tile(2, 0, 1, (2, 1))
        quantize_w(1, 0)
        round_mi(8)
        quantize_f(0, 0)
        copy_turned(0, 2)
        copy_turned(0, 3)
        pump()
        quantize_f(0, 1)
        quantize_w(1, 1)
        interleave_x(0)
        copy_turned(1, 0)
        copy_turned(1, 1)
        pump()
        copy_turned(1, 2)
        copy_turned(1, 3)
        interleave_g(0, 0)
        dx_steps(3)
        transpose_tile(2, 1, 7, (2, 2))
        transpose_tile(2, 2, 0, (2, 3))
        dx_steps(2)
        quantize_f(1, 0)
        copy_turned(2, 0)
        transpose_tile(2, 3, 1, (3, 0))
        pump()
        quantize_f(1, 1)
        quantize_t(0, 0)
        quantize_x(0)
        interleave_x(1)
        interleave_g(0, 1)
        copy_turned(2, 1)
        copy_turned(2, 2)
        copy_turned(2, 3)
        dx_steps(5)
        transpose_tile(3, 0, 7, (3, 1))
        transpose_tile(3, 1, 0, (3, 2))
        column_sums(3, 3)
        interleave_g(0, 2)
        quantize_t(0, 1)
        quantize_f(2, 0)
        quantize_x(1)
        interleave_x(2)
        copy_turned(3, 0)
        copy_turned(3, 1)
        copy_sums()
        interleave_g(0, 3)
        dx_steps(5)
        turn_sums()
        transpose_tile(3, 2, 1)
        transpose_tile(3, 3, 7)
        quantize_f(2, 1)
        pump()
        quantize_t(0, 2)
        quantize_x(2)
        interleave_x(3)
        pick_sums()
        interleave_g(1, 0)
        dx_steps(5)
        product_c(0, range(3))
        quantize_t(0, 3)
        quantize_x(3)
        product_c(0, range(3, 4))
        product_c(1)
        copy_turned(3, 2)
        copy_turned(3, 3)
        interleave_g(1, 1)
        dx_steps(1)
        dm_centre(0)
        product_c(2)
        product_c(3)
        dx_steps(2)
        dm_scale(0, nc.gpsimd)
        quantize_f(3, 0)
        pump()
        quantize_t(1, 0)
        interleave_g(1, 2)
        quantize_f(3, 1)
        quantize_t(1, 1)
        interleave_g(1, 3)
        dm_centre(1)
        dm_centre(2)
        dm_centre(3)
        dm_scale(1, nc.gpsimd)
        product_c(4, range(2))
        product_c(5, range(2))
        dx_steps(2)
        dm_scale(2, nc.gpsimd)
        product_c(6, range(2))
        product_c(7, range(2))
        dx_steps(2, 29)
        dm_scale(3, nc.gpsimd)
        quantize_t(1, 2)
        quantize_t(1, 3)
        product_c(4, range(2, 4))
        product_c(5, range(2, 4))
        dx_steps(1, 30)
        dm_centre(4)
        pump()
        dm_centre(5)
        dx_steps(1, 31)
        dm_scale(4, nc.gpsimd)
        product_c(6, range(2, 4))
        dx_steps(2)
        dm_scale(5, nc.gpsimd)
        product_c(7, range(2, 4))
        dm_centre(6)
        dx_steps(1)
        dm_scale(6, nc.gpsimd)
        dm_centre(7)
        dm_scale(7, nc.vector)
